import numpy as np
import ml_dtypes


def mxq(x, axis, fmt="e4m3"):
    dtype, down = {"e4m3": (ml_dtypes.float8_e4m3fn, 7), "e5m2": (ml_dtypes.float8_e5m2, 14)}[fmt]
    v = np.moveaxis(np.asarray(x, np.float32).astype(ml_dtypes.bfloat16).astype(np.float64), axis, -1)
    blocks = v.reshape(v.shape[:-1] + (-1, 32))
    amax = np.abs(blocks).max(-1, keepdims=True)
    byte = np.maximum(np.where(amax > 0, np.frexp(amax)[1] - 1 + 127, 0) - down, 1)
    scale = np.exp2(byte - 127.0)
    codes = (blocks / scale).astype(np.float32).astype(dtype).astype(np.float64)
    return np.moveaxis((codes * scale).reshape(v.shape), -1, axis)


WIDE = False


def mx_kscale(k):
    if not WIDE:
        return np.ones(k)
    levels = np.array([10, -10, 5, -5, 0])
    if k % 512:
        return np.exp2(np.random.permutation(np.resize(levels, k // 32))).repeat(32)
    a = np.empty((k // 512, 16))
    for p in range(k // 512):
        a[p, :8] = np.random.permutation(np.resize(levels, 8))
        for g in range(8):
            far = levels[np.abs(levels - a[p, g]) >= 10]
            a[p, g + 8] = far[np.random.randint(len(far))]
    return np.exp2(a.ravel()).repeat(32)


BF16 = ml_dtypes.bfloat16


def bf(x):
    return np.asarray(x, np.float32).astype(BF16)


def f64(x):
    return np.asarray(x).astype(np.float64)


B, H, L, D, C = 1, 8, 2048, 128, 512


def decay_block(i0, n):
    head_idx = np.arange(H, dtype=np.float64)
    gamma = 1.0 - np.exp2(-5.0 - head_idx)
    log2_gamma = np.log2(gamma)
    pos_diff = np.arange(i0, i0 + C, dtype=np.float64)[:, None] - np.arange(n, dtype=np.float64)[None, :]
    causal = np.where(pos_diff >= 0, 1.0, 0.0)
    return np.exp2(pos_diff[None] * log2_gamma[:, None, None]) * causal[None]


def setup_inputs():
    s = mx_kscale(L)
    return {"q_scaled": bf(np.random.standard_normal((B, H, L, D)) / np.sqrt(D)),
            "k": bf(np.random.standard_normal((B, H, L, D)) * s[:, None]),
            "v": bf(np.random.standard_normal((B, H, L, D)) * 0.25 / s[:, None])}


def reference(q_scaled, k, v):
    vq = mxq(f64(v), 2, "e4m3")
    out = np.zeros((B, H, L, D))
    for i0 in range(0, L, C):
        n = i0 + C
        scores = f64(q_scaled)[:, :, i0:n] @ f64(k)[:, :, :n].transpose(0, 1, 3, 2)
        p = scores * decay_block(i0, n)[None]
        out[:, :, i0:n] = mxq(p, 3, "e4m3") @ vq[:, :, :n]
    return out

@@ -1,0 +1,275 @@
+import math
+from contextlib import ExitStack
+
+import concourse.mybir as mybir
+from concourse.masks import make_identity
+
+BF16 = mybir.dt.bfloat16
+F32 = mybir.dt.float32
+I32 = mybir.dt.int32
+U32 = mybir.dt.uint32
+U8 = mybir.dt.uint8
+FP8X4 = mybir.dt.float8_e4m3fn_x4
+MULT = mybir.AluOpType.mult
+COPY = mybir.ActivationFunctionType.Copy
+EXP = mybir.ActivationFunctionType.Exp
+
+HEADS = 8
+SEQ = 2048
+D = 128
+P = 128
+PACK = 4
+CHUNK = P * PACK
+N_CHUNKS = SEQ // CHUNK
+BLOCKS = SEQ // P
+
+SHIFT = CHUNK - 1
+
+BANKS = 2 * PACK
+KEYS_OF_BLOCK = P // PACK
+
+LOADS_AHEAD = 2 * N_CHUNKS
+LAG = PACK
+
+FLOPS = 2 * 2 * HEADS * D * sum(CHUNK * CHUNK * (r + 1) for r in range(N_CHUNKS))
+
+
+def tile_model_pa_kernel(tc, q_scaled, k, v, out):
+    nc = tc.nc
+    gammas = [1.0 - 2.0 ** (-5 - h) for h in range(HEADS)]
+
+    with ExitStack() as ctx:
+        ctx.enter_context(tc.manual_schedule())
+        const = ctx.enter_context(tc.tile_pool(name="const", bufs=1))
+        raw = ctx.enter_context(tc.tile_pool(name="raw", bufs=LOADS_AHEAD // N_CHUNKS + 2))
+        per_head = ctx.enter_context(tc.tile_pool(name="per_head", bufs=2))
+        per_chunk = ctx.enter_context(tc.tile_pool(name="per_chunk", bufs=5))
+        work = ctx.enter_context(tc.tile_pool(name="work", bufs=3))
+        psum_vector = ctx.enter_context(tc.psum_pool(name="psum_vector", bufs=4))
+        psum_scalar = ctx.enter_context(tc.psum_pool(name="psum_scalar", bufs=4))
+
+        k_raw, q_raw, v_raw = {}, {}, {}
+
+        def load_chunk(h, c):
+            if c == 0:
+                k_raw[h] = raw.tile([P, BLOCKS, D], BF16, name="k_raw")
+                q_raw[h] = raw.tile([P, BLOCKS, D], BF16, name="q_raw")
+                v_raw[h] = raw.tile([P, BLOCKS, D], BF16, name="v_raw")
+            for rows, source, order in (
+                (k_raw[h], k, "(p b) d -> p b d"),
+                (q_raw[h], q_scaled, "(b p) d -> p b d"),
+                (v_raw[h], v, "(p b) d -> p b d"),
+            ):
+                nc.sync.dma_start(
+                    out=rows[:, PACK * c : PACK * (c + 1), :],
+                    in_=source[0, h, CHUNK * c : CHUNK * (c + 1), :].rearrange(order, p=P),
+                )
+
+        chunks = [(h, r) for h in range(HEADS) for r in range(N_CHUNKS)]
+        for chunk in chunks[0:LOADS_AHEAD]:
+            load_chunk(*chunk)
+
+        def exponents(shape, pattern, base, channel_multiplier, label):
+            as_i32 = const.tile(shape, I32, name=label + "_i32")
+            nc.gpsimd.iota(as_i32[:], pattern=pattern, base=base, channel_multiplier=channel_multiplier)
+            as_f32 = const.tile(shape, F32, name=label)
+            nc.vector.tensor_copy(out=as_f32[:], in_=as_i32[:])
+            return as_f32
+
+        table_exponent = exponents([P, P, PACK], [[1, P], [-1, PACK]], SHIFT, -PACK, "table_exponent")
+        identity = const.tile([P, P], BF16)
+        make_identity(nc, identity[:])
+        query_exponent = exponents([P, PACK], [[-1, PACK]], 0, 1, "query_exponent")
+        key_exponent = exponents([P, PACK], [[P, PACK]], 0, -PACK, "key_exponent")
+        identity_f32 = const.tile([P, P], F32)
+        make_identity(nc, identity_f32[:])
+        diagonal_tiles = []
+        for i in range(2):
+            zeroed = const.tile([P, PACK, P, PACK], BF16, name="diagonal%d" % i, align_bytes=64)
+            nc.vector.memset(zeroed[:], 0.0)
+            diagonal_tiles.append(zeroed)
+
+        k_t, q_t, decay, query_factor, key_factor = {}, {}, {}, {}, {}
+        v_grouped, v_codes, v_scales, p_codes, p_scales = {}, {}, {}, {}, {}
+
+        def power_of_gamma(h, exponent, label):
+            power = per_head.tile(list(exponent.shape), F32, name=label)
+            nc.scalar.activation(out=power[:], in_=exponent[:], func=EXP, scale=math.log(gammas[h]))
+            return power
+
+        def start_head(h):
+            k_t[h] = per_head.tile([P, SEQ], BF16, name="k_t")
+            q_t[h] = per_head.tile([P, SEQ], BF16, name="q_t")
+            v_grouped[h] = per_head.tile([P, N_CHUNKS, D, PACK], BF16, name="v_grouped", align_bytes=64)
+            v_codes[h] = per_head.tile([P, N_CHUNKS, D], U32, name="v_codes", align_bytes=64)
+            v_scales[h] = per_head.tile([P, N_CHUNKS, D], U8, name="v_scales", align_bytes=64)
+            decay[h] = power_of_gamma(h, table_exponent, "decay")
+            query_factor[h] = power_of_gamma(h, query_exponent, "query_factor")
+            key_factor[h] = power_of_gamma(h, key_exponent, "key_factor")
+
+        def transpose_chunk(rows, transposed, c):
+            flipped = psum_scalar.tile([P, PACK, P], BF16, tag="bank")
+            for b in range(PACK):
+                nc.tensor.transpose(out=flipped[:, b, :], in_=rows[:, PACK * c + b, :], identity=identity[:])
+            nc.scalar.copy(
+                out=transposed[:, c * CHUNK : (c + 1) * CHUNK], in_=flipped[:].rearrange("p b x -> p (b x)")
+            )
+
+        def prepare_chunk(h, c):
+            if c == 0:
+                start_head(h)
+            transpose_chunk(k_raw[h], k_t[h], c)
+            transpose_chunk(q_raw[h], q_t[h], c)
+            nc.gpsimd.tensor_scalar(
+                out=v_grouped[h][:, c, :, :],
+                in0=v_raw[h][:, PACK * c : PACK * (c + 1), :].rearrange("p t d -> p d t"),
+                scalar1=1.0,
+                scalar2=0.0,
+                op0=MULT,
+                op1=mybir.AluOpType.add,
+            )
+
+        def quantise_v(h, c):
+            nc.vector.quantize_mx(
+                out=v_codes[h][:, c, :].bitcast(FP8X4),
+                scales=v_scales[h][:, c, :],
+                in_=v_grouped[h][:, c, :, :].rearrange("p d t -> p (d t)"),
+            )
+
+        def block(transposed, index):
+            return transposed[:, index * P : (index + 1) * P]
+
+
+        def vector_block(h, r, g, b, grouped):
+            scores_t = psum_vector.tile([P, PACK, P], F32)
+            for t in range(PACK):
+                nc.tensor.matmul(
+                    out=scores_t[:, t, :],
+                    lhsT=block(k_t[h], PACK * g + t),
+                    rhs=block(q_t[h], PACK * r + b),
+                    start=True,
+                    stop=True,
+                )
+            distance = CHUNK * (r - g) + P * b
+            nc.vector.scalar_tensor_tensor(
+                out=grouped[:, b, :, :],
+                in0=scores_t[:].rearrange("p t i -> p i t"),
+                scalar=gammas[h] ** (distance - SHIFT),
+                in1=decay[h][:],
+                op0=MULT,
+                op1=MULT,
+            )
+
+        def by_key(h, r, t, half_done):
+            scores = psum_scalar.tile([P, PACK, P], F32, tag="bank")
+            for b in range(PACK):
+                nc.tensor.matmul(
+                    out=scores[:, b, :],
+                    lhsT=block(q_t[h], PACK * r + b),
+                    rhs=block(k_t[h], PACK * r + t),
+                    start=True,
+                    stop=True,
+                )
+            nc.scalar.activation(
+                out=half_done[:, CHUNK * t : CHUNK * (t + 1)],
+                in_=scores[:].rearrange("p b x -> p (b x)"),
+                func=COPY,
+                scale=query_factor[h][:, t : t + 1],
+            )
+            pitch = P + KEYS_OF_BLOCK
+            own = half_done[:, CHUNK * t : CHUNK * t + PACK * pitch].rearrange("p (b y) -> p b y", y=pitch)
+            nc.gpsimd.affine_select(
+                out=own[:, :, 0:KEYS_OF_BLOCK],
+                in_=own[:, :, 0:KEYS_OF_BLOCK],
+                pattern=[[0, PACK], [-PACK, KEYS_OF_BLOCK]],
+                compare_op=mybir.AluOpType.is_ge,
+                fill=0.0,
+                base=-t,
+                channel_multiplier=1,
+            )
+
+        def by_query_block(h, b, half_done, grouped):
+            flipped = psum_scalar.tile([P, PACK, P], F32, tag="bank")
+            for t in range(PACK):
+                first = CHUNK * t + P * b
+                nc.tensor.transpose(out=flipped[:, t, :], in_=half_done[:, first : first + P], identity=identity_f32[:])
+            words = KEYS_OF_BLOCK * (b + 1)
+            nc.scalar.activation(
+                out=grouped[0:words, b, :, :],
+                in_=flipped[0:words, :, :].rearrange("p t i -> p i t"),
+                func=COPY,
+                scale=key_factor[h][0:words, b : b + 1],
+            )
+
+        def quantise_scores(h, r, g, grouped):
+            if (h, r) not in p_codes:
+                p_codes[h, r] = per_chunk.tile([P, N_CHUNKS, CHUNK], U32, name="p_codes", align_bytes=64)
+                p_scales[h, r] = per_chunk.tile([P, N_CHUNKS, CHUNK], U8, name="p_scales", align_bytes=64)
+            nc.vector.quantize_mx(
+                out=p_codes[h, r][:, g, :].bitcast(FP8X4),
+                scales=p_scales[h, r][:, g, :],
+                in_=grouped[:].rearrange("p b i t -> p (b i t)"),
+            )
+
+        def weighted_values(h, r):
+            acc = psum_scalar.tile([P, PACK, D], F32, tag="bank")
+            for b in range(PACK):
+                queries = slice(b * P, (b + 1) * P)
+                for g in range(r + 1):
+                    nc.tensor.matmul_mx(
+                        out=acc[:, b, :],
+                        lhsT=p_codes[h, r][:, g, queries].bitcast(FP8X4),
+                        lhsT_scale=p_scales[h, r][:, g, queries],
+                        rhs=v_codes[h][:, g, :].bitcast(FP8X4),
+                        rhs_scale=v_scales[h][:, g, :],
+                        start=(g == 0),
+                        stop=(g == r),
+                    )
+            result = work.tile([P, PACK, D], F32)
+            nc.scalar.copy(out=result[:], in_=acc[:])
+            nc.sync.dma_start(
+                out=out[0, h, r * CHUNK : (r + 1) * CHUNK, :].rearrange("(b p) d -> p b d", p=P), in_=result[:]
+            )
+
+        vector_blocks = [
+            (h, r, g, b) for h in range(HEADS) for r in range(N_CHUNKS) for g in range(r) for b in range(PACK)
+        ]
+        to_quantise = {}
+        to_multiply = {}
+        batches_left = {(h, r): r + 1 for (h, r) in chunks}
+        half_done = {}
+        grouped = None
+        for step in range(-2 * BANKS, BANKS * len(chunks) + BANKS + 2 * LAG + 1):
+            turn, phase = divmod(step, 4)
+            if phase < 3 and 0 <= 3 * turn + phase < len(vector_blocks):
+                h, r, g, b = vector_blocks[3 * turn + phase]
+                if b == 0:
+                    grouped = work.tile([P, PACK, P, PACK], BF16, name="grouped", align_bytes=64)
+                vector_block(h, r, g, b, grouped)
+                if b == PACK - 1:
+                    to_quantise[step + LAG] = to_quantise.get(step + LAG, []) + [(h, r, g, grouped)]
+
+            y, bank = divmod(step, BANKS)
+            if bank == 0 and 0 <= y + 2 < len(chunks):
+                prepare_chunk(*chunks[y + 2])
+                if y + 2 + LOADS_AHEAD < len(chunks):
+                    load_chunk(*chunks[y + 2 + LOADS_AHEAD])
+            if bank == PACK and 0 <= y < len(chunks):
+                quantise_v(*chunks[y])
+            if bank < PACK and 0 <= y < len(chunks):
+                if bank == 0:
+                    half_done[y] = work.tile([P, PACK * CHUNK + P], F32, name="half_done", bufs=2)
+                by_key(*chunks[y], bank, half_done[y])
+            if bank >= PACK and 0 <= y - 1 < len(chunks):
+                h, r = chunks[y - 1]
+                by_query_block(h, bank - PACK, half_done[y - 1], diagonal_tiles[y % 2])
+                if bank == BANKS - 1:
+                    to_quantise[step + LAG] = to_quantise.get(step + LAG, []) + [(h, r, r, diagonal_tiles[y % 2])]
+
+            for chunk in to_multiply.get(step, []):
+                weighted_values(*chunk)
+            for h, r, g, written in to_quantise.get(step, []):
+                quantise_scores(h, r, g, written)
+                batches_left[h, r] -= 1
+                if batches_left[h, r] == 0:
+                    to_multiply[step + LAG] = to_multiply.get(step + LAG, []) + [(h, r)]

@@ -22,14 +22,21 @@ PACK = 4
 CHUNK = P * PACK
 N_CHUNKS = SEQ // CHUNK
 BLOCKS = SEQ // P
+QUARTER = P // PACK
 
 SHIFT = CHUNK - 1
 
-BANKS = 2 * PACK
-KEYS_OF_BLOCK = P // PACK
+SETS = (
+    ((0, 3, 0),),
+    ((1, 3, 0),),
+    ((0, 2, 0), (0, 0, 3 * QUARTER)),
+    ((1, 2, 0), (1, 0, 3 * QUARTER)),
+    ((0, 1, 0), (1, 1, 2 * QUARTER)),
+)
+N_SETS = len(SETS)
 
 LOADS_AHEAD = 2 * N_CHUNKS
-LAG = PACK
+STEPS = 12
 
 FLOPS = 2 * 2 * HEADS * D * sum(CHUNK * CHUNK * (r + 1) for r in range(N_CHUNKS))
 
@@ -66,31 +73,51 @@ def tile_model_pa_kernel(tc, q_scaled, k, v, out):
                 )
 
         chunks = [(h, r) for h in range(HEADS) for r in range(N_CHUNKS)]
+        pairs = [(h, r) for h in range(HEADS) for r in range(0, N_CHUNKS, 2)]
         for chunk in chunks[0:LOADS_AHEAD]:
             load_chunk(*chunk)
 
-        def exponents(shape, pattern, base, channel_multiplier, label):
+        def exponents(shape, label, pieces):
             as_i32 = const.tile(shape, I32, name=label + "_i32")
-            nc.gpsimd.iota(as_i32[:], pattern=pattern, base=base, channel_multiplier=channel_multiplier)
+            for part, pattern, base, channel_multiplier in pieces:
+                nc.gpsimd.iota(as_i32[part], pattern=pattern, base=base, channel_multiplier=channel_multiplier)
             as_f32 = const.tile(shape, F32, name=label)
             nc.vector.tensor_copy(out=as_f32[:], in_=as_i32[:])
             return as_f32
 
-        table_exponent = exponents([P, P, PACK], [[1, P], [-1, PACK]], SHIFT, -PACK, "table_exponent")
+        every = slice(None)
+        table_exponent = exponents(
+            [P, P, PACK], "table_exponent", [((every,), [[1, P], [-1, PACK]], SHIFT, -PACK)]
+        )
         identity = const.tile([P, P], BF16)
         make_identity(nc, identity[:])
-        query_exponent = exponents([P, PACK], [[-1, PACK]], 0, 1, "query_exponent")
-        key_exponent = exponents([P, PACK], [[P, PACK]], 0, -PACK, "key_exponent")
+        query_exponent = exponents([P, PACK], "query_exponent", [((every,), [[-1, PACK]], 0, 1)])
+        key_exponent = exponents(
+            [P, N_SETS],
+            "key_exponent",
+            [
+                ((slice(first, P), slice(s, s + 1)), [[0, 1]], P * b, -PACK)
+                for s in range(N_SETS)
+                for pos, b, first in SETS[s]
+            ],
+        )
         identity_f32 = const.tile([P, P], F32)
         make_identity(nc, identity_f32[:])
-        diagonal_tiles = []
-        for i in range(2):
-            zeroed = const.tile([P, PACK, P, PACK], BF16, name="diagonal%d" % i, align_bytes=64)
-            nc.vector.memset(zeroed[:], 0.0)
-            diagonal_tiles.append(zeroed)
+
+        v_012, v_0, v_01, v_0_scales, v_01_scales = [], [], [], [], []
+        for parity in range(2):
+            for tiles, label in ((v_012, "v_012"), (v_0, "v_0"), (v_01, "v_01")):
+                zeroed = const.tile([P, N_CHUNKS, D], U32, name="%s_%d" % (label, parity), align_bytes=64)
+                nc.vector.memset(zeroed[:], 0)
+                tiles.append(zeroed)
+            for tiles, label in ((v_0_scales, "v_0_scales"), (v_01_scales, "v_01_scales")):
+                zeroed = const.tile([P, N_CHUNKS, D], U8, name="%s_%d" % (label, parity), align_bytes=64)
+                nc.vector.memset(zeroed[:].bitcast(I32), 0)
+                tiles.append(zeroed)
 
         k_t, q_t, decay, query_factor, key_factor = {}, {}, {}, {}, {}
         v_grouped, v_codes, v_scales, p_codes, p_scales = {}, {}, {}, {}, {}
+        half_done, packed, packed_codes, packed_scales = {}, {}, {}, {}
 
         def power_of_gamma(h, exponent, label):
             power = per_head.tile(list(exponent.shape), F32, name=label)
@@ -135,6 +162,22 @@ def tile_model_pa_kernel(tc, q_scaled, k, v, out):
                 scales=v_scales[h][:, c, :],
                 in_=v_grouped[h][:, c, :, :].rearrange("p d t -> p (d t)"),
             )
+            n, two, three = h % 2, 2 * QUARTER, 3 * QUARTER
+            moves = [
+                (v_012[n][0:three, c, :], v_codes[h][0:three, c, :]),
+                (v_0[n][three:P, c, :], v_codes[h][0:QUARTER, c, :]),
+                (v_0_scales[n][three : three + 4, c, :], v_scales[h][0:4, c, :]),
+            ]
+            if c % 2 == 0:
+                moves += [(v_01[n][0:two, c, :], v_codes[h][0:two, c, :])]
+            else:
+                moves += [
+                    (v_01[n][two:P, c, :], v_codes[h][0:two, c, :]),
+                    (v_01_scales[n][two : two + 4, c, :], v_scales[h][0:4, c, :]),
+                    (v_01_scales[n][three : three + 4, c, :], v_scales[h][QUARTER : QUARTER + 4, c, :]),
+                ]
+            for target, source in moves:
+                nc.sync.dma_start(out=target.bitcast(I32), in_=source.bitcast(I32))
 
         def block(transposed, index):
             return transposed[:, index * P : (index + 1) * P]
@@ -160,72 +203,103 @@ def tile_model_pa_kernel(tc, q_scaled, k, v, out):
                 op1=MULT,
             )
 
-        def by_key(h, r, t, half_done):
+        def first_trip(h, r, columns, half_done):
             scores = psum_scalar.tile([P, PACK, P], F32, tag="bank")
-            for b in range(PACK):
-                nc.tensor.matmul(
-                    out=scores[:, b, :],
-                    lhsT=block(q_t[h], PACK * r + b),
-                    rhs=block(k_t[h], PACK * r + t),
-                    start=True,
-                    stop=True,
+            for place, (s, t) in enumerate(columns):
+                for pos, b, first in SETS[s]:
+                    words = QUARTER * (b + 1)
+                    nc.tensor.matmul(
+                        out=scores[:, place, first : first + words],
+                        lhsT=block(q_t[h], PACK * (r + pos) + b),
+                        rhs=block(k_t[h], PACK * (r + pos) + t)[:, 0:words],
+                        start=True,
+                        stop=True,
+                    )
+            place = 0
+            while place < PACK:
+                s, t = columns[place]
+                alike = len([c for c in columns if c[1] == t])
+                nc.scalar.activation(
+                    out=half_done[:, t, s : s + alike, :],
+                    in_=scores[:, place : place + alike, :],
+                    func=COPY,
+                    scale=query_factor[h][:, t : t + 1],
                 )
-            nc.scalar.activation(
-                out=half_done[:, CHUNK * t : CHUNK * (t + 1)],
-                in_=scores[:].rearrange("p b x -> p (b x)"),
-                func=COPY,
-                scale=query_factor[h][:, t : t + 1],
-            )
-            pitch = P + KEYS_OF_BLOCK
-            own = half_done[:, CHUNK * t : CHUNK * t + PACK * pitch].rearrange("p (b y) -> p b y", y=pitch)
+                place += alike
+
+        def mask_own_keys(own, t):
             nc.gpsimd.affine_select(
-                out=own[:, :, 0:KEYS_OF_BLOCK],
-                in_=own[:, :, 0:KEYS_OF_BLOCK],
-                pattern=[[0, PACK], [-PACK, KEYS_OF_BLOCK]],
+                out=own,
+                in_=own,
+                pattern=[[-1 if t is None else 0, own.shape[1]], [-PACK, QUARTER]],
                 compare_op=mybir.AluOpType.is_ge,
                 fill=0.0,
-                base=-t,
+                base=0 if t is None else -t,
                 channel_multiplier=1,
             )
 
-        def by_query_block(h, b, half_done, grouped):
+        def second_trip(h, s, half_done, packed):
             flipped = psum_scalar.tile([P, PACK, P], F32, tag="bank")
             for t in range(PACK):
-                first = CHUNK * t + P * b
-                nc.tensor.transpose(out=flipped[:, t, :], in_=half_done[:, first : first + P], identity=identity_f32[:])
-            words = KEYS_OF_BLOCK * (b + 1)
+                nc.tensor.transpose(out=flipped[:, t, :], in_=half_done[:, t, s, :], identity=identity_f32[:])
             nc.scalar.activation(
-                out=grouped[0:words, b, :, :],
-                in_=flipped[0:words, :, :].rearrange("p t i -> p i t"),
+                out=packed[:, s, :, :],
+                in_=flipped[:].rearrange("p t i -> p i t"),
                 func=COPY,
-                scale=key_factor[h][0:words, b : b + 1],
+                scale=key_factor[h][:, s : s + 1],
             )
 
         def quantise_scores(h, r, g, grouped):
             if (h, r) not in p_codes:
-                p_codes[h, r] = per_chunk.tile([P, N_CHUNKS, CHUNK], U32, name="p_codes", align_bytes=64)
-                p_scales[h, r] = per_chunk.tile([P, N_CHUNKS, CHUNK], U8, name="p_scales", align_bytes=64)
+                p_codes[h, r] = per_chunk.tile([P, N_CHUNKS - 1, CHUNK], U32, name="p_codes", align_bytes=64)
+                p_scales[h, r] = per_chunk.tile([P, N_CHUNKS - 1, CHUNK], U8, name="p_scales", align_bytes=64)
             nc.vector.quantize_mx(
                 out=p_codes[h, r][:, g, :].bitcast(FP8X4),
                 scales=p_scales[h, r][:, g, :],
                 in_=grouped[:].rearrange("p b i t -> p (b i t)"),
             )
 
-        def weighted_values(h, r):
+        def quantise_sets(y, sets):
+            if y not in packed_codes:
+                packed_codes[y] = work.tile([P, N_SETS, P], U32, name="packed_codes", align_bytes=64)
+                packed_scales[y] = work.tile([P, N_SETS, P], U8, name="packed_scales", align_bytes=64)
+            nc.vector.quantize_mx(
+                out=packed_codes[y][:, sets, :].rearrange("p s i -> p (s i)").bitcast(FP8X4),
+                scales=packed_scales[y][:, sets, :].rearrange("p s i -> p (s i)"),
+                in_=packed[y][:, sets, :, :].rearrange("p s i t -> p (s i t)"),
+            )
+
+        def weighted_values(y, h, r):
+            pos, n = r % 2, h % 2
+            on_diagonal = {
+                3: (pos, v_codes[h], v_scales[h]),
+                2: (2 + pos, v_012[n], v_scales[h]),
+                1: (4, v_01[n], v_01_scales[n] if pos else v_scales[h]),
+                0: (2 + pos, v_0[n], v_0_scales[n]),
+            }
             acc = psum_scalar.tile([P, PACK, D], F32, tag="bank")
             for b in range(PACK):
                 queries = slice(b * P, (b + 1) * P)
                 for g in range(r + 1):
+                    if g < r:
+                        codes, scales = p_codes[h, r][:, g, queries], p_scales[h, r][:, g, queries]
+                        values, value_scales = v_codes[h], v_scales[h]
+                    else:
+                        s, values, value_scales = on_diagonal[b]
+                        codes, scales = packed_codes[y][:, s, :], packed_scales[y][:, s, :]
                     nc.tensor.matmul_mx(
                         out=acc[:, b, :],
-                        lhsT=p_codes[h, r][:, g, queries].bitcast(FP8X4),
-                        lhsT_scale=p_scales[h, r][:, g, queries],
-                        rhs=v_codes[h][:, g, :].bitcast(FP8X4),
-                        rhs_scale=v_scales[h][:, g, :],
+                        lhsT=codes.bitcast(FP8X4),
+                        lhsT_scale=scales,
+                        rhs=values[:, g, :].bitcast(FP8X4),
+                        rhs_scale=value_scales[:, g, :],
                         start=(g == 0),
                         stop=(g == r),
                     )
-            result = work.tile([P, PACK, D], F32)
+            return acc
+
+        def store(h, r, acc):
+            result = work.tile([P, PACK, D], F32, name="result")
             nc.scalar.copy(out=result[:], in_=acc[:])
             nc.sync.dma_start(
                 out=out[0, h, r * CHUNK : (r + 1) * CHUNK, :].rearrange("(b p) d -> p b d", p=P), in_=result[:]
@@ -234,42 +308,60 @@ def tile_model_pa_kernel(tc, q_scaled, k, v, out):
         vector_blocks = [
             (h, r, g, b) for h in range(HEADS) for r in range(N_CHUNKS) for g in range(r) for b in range(PACK)
         ]
+        prepared = 3
+        for chunk in chunks[0:prepared]:
+            prepare_chunk(*chunk)
+            quantise_v(*chunk)
+        acc = {}
         to_quantise = {}
-        to_multiply = {}
-        batches_left = {(h, r): r + 1 for (h, r) in chunks}
-        half_done = {}
-        grouped = None
-        for step in range(-2 * BANKS, BANKS * len(chunks) + BANKS + 2 * LAG + 1):
-            turn, phase = divmod(step, 4)
-            if phase < 3 and 0 <= 3 * turn + phase < len(vector_blocks):
-                h, r, g, b = vector_blocks[3 * turn + phase]
+        for step in range(STEPS * (len(pairs) + 1)):
+            y, n = divmod(step, STEPS)
+            if step < len(vector_blocks):
+                h, r, g, b = vector_blocks[step]
                 if b == 0:
                     grouped = work.tile([P, PACK, P, PACK], BF16, name="grouped", align_bytes=64)
                 vector_block(h, r, g, b, grouped)
                 if b == PACK - 1:
-                    to_quantise[step + LAG] = to_quantise.get(step + LAG, []) + [(h, r, g, grouped)]
+                    to_quantise[step + 1] = (h, r, g, grouped)
 
-            y, bank = divmod(step, BANKS)
-            if bank == 0 and 0 <= y + 2 < len(chunks):
-                prepare_chunk(*chunks[y + 2])
-                if y + 2 + LOADS_AHEAD < len(chunks):
-                    load_chunk(*chunks[y + 2 + LOADS_AHEAD])
-            if bank == PACK and 0 <= y < len(chunks):
-                quantise_v(*chunks[y])
-            if bank < PACK and 0 <= y < len(chunks):
-                if bank == 0:
-                    half_done[y] = work.tile([P, PACK * CHUNK + P], F32, name="half_done", bufs=2)
-                by_key(*chunks[y], bank, half_done[y])
-            if bank >= PACK and 0 <= y - 1 < len(chunks):
-                h, r = chunks[y - 1]
-                by_query_block(h, bank - PACK, half_done[y - 1], diagonal_tiles[y % 2])
-                if bank == BANKS - 1:
-                    to_quantise[step + LAG] = to_quantise.get(step + LAG, []) + [(h, r, r, diagonal_tiles[y % 2])]
+            if y < len(pairs):
+                h, r = pairs[y]
+                if n == 0:
+                    half_done[y] = work.tile([P, PACK, N_SETS, P], F32, name="half_done", bufs=2)
+                    packed[y] = work.tile([P, N_SETS, P, PACK], BF16, name="packed", bufs=2, align_bytes=64)
+                if n < PACK:
+                    first_trip(h, r, [(s, n) for s in range(PACK)], half_done[y])
+                    mask_own_keys(half_done[y][:, n, 0:PACK, 3 * QUARTER : P], n)
+                if n == PACK - 1:
+                    for s in (2, 3):
+                        mask_own_keys(half_done[y][:, :, s, 2 * QUARTER : 3 * QUARTER], None)
+                if n == PACK:
+                    first_trip(h, r, [(PACK, t) for t in range(PACK)], half_done[y])
+                    for quarter in (1, 3):
+                        own = slice(quarter * QUARTER, (quarter + 1) * QUARTER)
+                        mask_own_keys(half_done[y][:, :, PACK, own], None)
+                if n in (5, 6):
+                    c = prepared + 2 * y + n - 5
+                    if c < len(chunks):
+                        prepare_chunk(*chunks[c])
+                        if c - prepared + LOADS_AHEAD < len(chunks):
+                            load_chunk(*chunks[c - prepared + LOADS_AHEAD])
+                if n in (9, 10):
+                    c = prepared + 2 * y + n - 9
+                    if c < len(chunks):
+                        quantise_v(*chunks[c])
+                if n >= STEPS - N_SETS:
+                    second_trip(h, n - (STEPS - N_SETS), half_done[y], packed[y])
 
-            for chunk in to_multiply.get(step, []):
-                weighted_values(*chunk)
-            for h, r, g, written in to_quantise.get(step, []):
-                quantise_scores(h, r, g, written)
-                batches_left[h, r] -= 1
-                if batches_left[h, r] == 0:
-                    to_multiply[step + LAG] = to_multiply.get(step + LAG, []) + [(h, r)]
+            if y > 0:
+                h, r = pairs[y - 1]
+                if n == 0:
+                    quantise_sets(y - 1, slice(0, PACK))
+                if n == 1:
+                    quantise_sets(y - 1, slice(PACK, N_SETS))
+                if n in (5, 7):
+                    acc[n] = weighted_values(y - 1, h, r + (n - 5) // 2)
+                if n in (6, 9):
+                    store(h, r + (n - 6) // 3, acc[5 if n == 6 else 7])
+            if step in to_quantise:
+                quantise_scores(*to_quantise[step])

@@ -55,26 +55,31 @@ def tile_model_pa_kernel(tc, q_scaled, k, v, out):
         psum_vector = ctx.enter_context(tc.psum_pool(name="psum_vector", bufs=4))
         psum_scalar = ctx.enter_context(tc.psum_pool(name="psum_scalar", bufs=4))
 
-        k_raw, q_raw, v_raw = {}, {}, {}
+        sources = {"k": (k, "(p b) d -> p b d"), "q": (q_scaled, "(b p) d -> p b d"), "v": (v, "(p b) d -> p b d")}
+        rows = {}
+
+        def load(which, h, c):
+            if (which, h) not in rows:
+                rows[which, h] = raw.tile([P, BLOCKS, D], BF16, name=which + "_raw")
+            source, order = sources[which]
+            nc.sync.dma_start(
+                out=rows[which, h][:, PACK * c : PACK * (c + 1), :],
+                in_=source[0, h, CHUNK * c : CHUNK * (c + 1), :].rearrange(order, p=P),
+            )
 
         def load_chunk(h, c):
-            if c == 0:
-                k_raw[h] = raw.tile([P, BLOCKS, D], BF16, name="k_raw")
-                q_raw[h] = raw.tile([P, BLOCKS, D], BF16, name="q_raw")
-                v_raw[h] = raw.tile([P, BLOCKS, D], BF16, name="v_raw")
-            for rows, source, order in (
-                (k_raw[h], k, "(p b) d -> p b d"),
-                (q_raw[h], q_scaled, "(b p) d -> p b d"),
-                (v_raw[h], v, "(p b) d -> p b d"),
-            ):
-                nc.sync.dma_start(
-                    out=rows[:, PACK * c : PACK * (c + 1), :],
-                    in_=source[0, h, CHUNK * c : CHUNK * (c + 1), :].rearrange(order, p=P),
-                )
+            for which in ("k", "q", "v"):
+                load(which, h, c)
 
         chunks = [(h, r) for h in range(HEADS) for r in range(N_CHUNKS)]
         pairs = [(h, r) for h in range(HEADS) for r in range(0, N_CHUNKS, 2)]
-        for chunk in chunks[0:LOADS_AHEAD]:
+        load("k", 0, 0)
+        load("q", 0, 1)
+        load("q", 0, 0)
+        load("k", 0, 1)
+        load("v", 0, 0)
+        load("v", 0, 1)
+        for chunk in chunks[2:LOADS_AHEAD]:
             load_chunk(*chunk)
 
         def exponents(shape, label, pieces):
@@ -134,10 +139,13 @@ def tile_model_pa_kernel(tc, q_scaled, k, v, out):
             query_factor[h] = power_of_gamma(h, query_exponent, "query_factor")
             key_factor[h] = power_of_gamma(h, key_exponent, "key_factor")
 
-        def transpose_chunk(rows, transposed, c):
+        def transpose_chunk(which, h, c):
+            transposed = (k_t if which == "k" else q_t)[h]
             flipped = psum_scalar.tile([P, PACK, P], BF16, tag="bank")
             for b in range(PACK):
-                nc.tensor.transpose(out=flipped[:, b, :], in_=rows[:, PACK * c + b, :], identity=identity[:])
+                nc.tensor.transpose(
+                    out=flipped[:, b, :], in_=rows[which, h][:, PACK * c + b, :], identity=identity[:]
+                )
             nc.scalar.copy(
                 out=transposed[:, c * CHUNK : (c + 1) * CHUNK], in_=flipped[:].rearrange("p b x -> p (b x)")
             )
@@ -145,11 +153,14 @@ def tile_model_pa_kernel(tc, q_scaled, k, v, out):
         def prepare_chunk(h, c):
             if c == 0:
                 start_head(h)
-            transpose_chunk(k_raw[h], k_t[h], c)
-            transpose_chunk(q_raw[h], q_t[h], c)
+            transpose_chunk("k", h, c)
+            transpose_chunk("q", h, c)
+            group_v(h, c)
+
+        def group_v(h, c):
             nc.gpsimd.tensor_scalar(
                 out=v_grouped[h][:, c, :, :],
-                in0=v_raw[h][:, PACK * c : PACK * (c + 1), :].rearrange("p t d -> p d t"),
+                in0=rows["v", h][:, PACK * c : PACK * (c + 1), :].rearrange("p t d -> p d t"),
                 scalar1=1.0,
                 scalar2=0.0,
                 op0=MULT,
@@ -184,7 +195,7 @@ def tile_model_pa_kernel(tc, q_scaled, k, v, out):
 
 
         def vector_block(h, r, g, b, grouped):
-            scores_t = psum_vector.tile([P, PACK, P], F32)
+            scores_t = psum_vector.tile([P, PACK, P], F32, name="scores_t")
             for t in range(PACK):
                 nc.tensor.matmul(
                     out=scores_t[:, t, :],
@@ -249,14 +260,14 @@ def tile_model_pa_kernel(tc, q_scaled, k, v, out):
                 scale=key_factor[h][:, s : s + 1],
             )
 
-        def quantise_scores(h, r, g, grouped):
+        def quantise_scores(h, r, g, grouped, blocks):
             if (h, r) not in p_codes:
                 p_codes[h, r] = per_chunk.tile([P, N_CHUNKS - 1, CHUNK], U32, name="p_codes", align_bytes=64)
                 p_scales[h, r] = per_chunk.tile([P, N_CHUNKS - 1, CHUNK], U8, name="p_scales", align_bytes=64)
             nc.vector.quantize_mx(
-                out=p_codes[h, r][:, g, :].bitcast(FP8X4),
-                scales=p_scales[h, r][:, g, :],
-                in_=grouped[:].rearrange("p b i t -> p (b i t)"),
+                out=p_codes[h, r][:, g, blocks.start * P : blocks.stop * P].bitcast(FP8X4),
+                scales=p_scales[h, r][:, g, blocks.start * P : blocks.stop * P],
+                in_=grouped[:, blocks, :, :].rearrange("p b i t -> p (b i t)"),
             )
 
         def quantise_sets(y, sets):
@@ -269,7 +280,10 @@ def tile_model_pa_kernel(tc, q_scaled, k, v, out):
                 in_=packed[y][:, sets, :, :].rearrange("p s i t -> p (s i t)"),
             )
 
-        def weighted_values(y, h, r):
+        def new_acc(blocks):
+            return psum_scalar.tile([P, len(blocks), D], F32, name="acc", tag="bank")
+
+        def weighted_values(y, h, r, blocks, turns, acc):
             pos, n = r % 2, h % 2
             on_diagonal = {
                 3: (pos, v_codes[h], v_scales[h]),
@@ -277,10 +291,10 @@ def tile_model_pa_kernel(tc, q_scaled, k, v, out):
                 1: (4, v_01[n], v_01_scales[n] if pos else v_scales[h]),
                 0: (2 + pos, v_0[n], v_0_scales[n]),
             }
-            acc = psum_scalar.tile([P, PACK, D], F32, tag="bank")
-            for b in range(PACK):
+            order = list(range(r - 1)) + [r] + list(range(max(r - 1, 0), r))
+            for place, b in enumerate(blocks):
                 queries = slice(b * P, (b + 1) * P)
-                for g in range(r + 1):
+                for g in order[turns]:
                     if g < r:
                         codes, scales = p_codes[h, r][:, g, queries], p_scales[h, r][:, g, queries]
                         values, value_scales = v_codes[h], v_scales[h]
@@ -288,80 +302,112 @@ def tile_model_pa_kernel(tc, q_scaled, k, v, out):
                         s, values, value_scales = on_diagonal[b]
                         codes, scales = packed_codes[y][:, s, :], packed_scales[y][:, s, :]
                     nc.tensor.matmul_mx(
-                        out=acc[:, b, :],
+                        out=acc[:, place, :],
                         lhsT=codes.bitcast(FP8X4),
                         lhsT_scale=scales,
                         rhs=values[:, g, :].bitcast(FP8X4),
                         rhs_scale=value_scales[:, g, :],
-                        start=(g == 0),
-                        stop=(g == r),
+                        start=(g == order[0]),
+                        stop=(g == order[-1]),
                     )
-            return acc
 
-        def store(h, r, acc):
-            result = work.tile([P, PACK, D], F32, name="result")
-            nc.scalar.copy(out=result[:], in_=acc[:])
+        def store(h, r, blocks, acc, copy):
+            result = work.tile([P, len(blocks), D], F32, name="result", bufs=6)
+            copy(out=result[:], in_=acc[:])
+            first = r * CHUNK + blocks[0] * P
             nc.sync.dma_start(
-                out=out[0, h, r * CHUNK : (r + 1) * CHUNK, :].rearrange("(b p) d -> p b d", p=P), in_=result[:]
+                out=out[0, h, first : first + len(blocks) * P, :].rearrange("(b p) d -> p b d", p=P), in_=result[:]
             )
 
         vector_blocks = [
             (h, r, g, b) for h in range(HEADS) for r in range(N_CHUNKS) for g in range(r) for b in range(PACK)
         ]
-        prepared = 3
-        for chunk in chunks[0:prepared]:
-            prepare_chunk(*chunk)
-            quantise_v(*chunk)
-        acc = {}
-        to_quantise = {}
+        last = len(pairs) - 1
+        every_block = range(PACK)
+        due = {}
+
+        def later(step, action, *arguments):
+            due.setdefault(step, []).append((action, arguments))
+
+        def multiply_and_store(step, delay, y, h, r):
+            acc = new_acc(every_block)
+            weighted_values(y, h, r, every_block, every, acc)
+            later(step + delay, store, h, r, every_block, acc, nc.scalar.copy)
+
+        def finish(y, h, r):
+            accs = [new_acc([b]) for b in every_block]
+            for b in every_block:
+                weighted_values(y, h, r + 1, [b], slice(0, r + 1), accs[b])
+            acc = psum_vector.tile([P, PACK, D], F32, name="scores_t")
+            weighted_values(y, h, r, every_block, every, acc)
+            store(h, r, every_block, acc, nc.scalar.copy)
+            for b in every_block:
+                weighted_values(y, h, r + 1, [b], slice(r + 1, r + 2), accs[b])
+            for b in every_block:
+                store(h, r + 1, [b], accs[b], nc.vector.tensor_copy if b % 2 else nc.scalar.copy)
+
+        start_head(0)
+        transpose_chunk("k", 0, 0)
+        transpose_chunk("q", 0, 1)
+        for c in range(2):
+            group_v(0, c)
+            later(2 + c, quantise_v, 0, c)
+
         for step in range(STEPS * (len(pairs) + 1)):
             y, n = divmod(step, STEPS)
             if step < len(vector_blocks):
                 h, r, g, b = vector_blocks[step]
                 if b == 0:
-                    grouped = work.tile([P, PACK, P, PACK], BF16, name="grouped", align_bytes=64)
+                    grouped = work.tile([P, PACK, P, PACK], BF16, name="grouped", bufs=4, align_bytes=64)
                 vector_block(h, r, g, b, grouped)
-                if b == PACK - 1:
-                    to_quantise[step + 1] = (h, r, g, grouped)
+                if step >= len(vector_blocks) - PACK:
+                    later(step + 1, quantise_scores, h, r, g, grouped, slice(b, b + 1))
+                elif b == PACK - 1:
+                    later(step + (1 + PACK if n < PACK else 1), quantise_scores, h, r, g, grouped, slice(0, PACK))
 
-            if y < len(pairs):
+            if step == 0:
+                transpose_chunk("q", 0, 0)
+                transpose_chunk("k", 0, 1)
+            if y <= last:
                 h, r = pairs[y]
                 if n == 0:
                     half_done[y] = work.tile([P, PACK, N_SETS, P], F32, name="half_done", bufs=2)
                     packed[y] = work.tile([P, N_SETS, P, PACK], BF16, name="packed", bufs=2, align_bytes=64)
-                if n < PACK:
-                    first_trip(h, r, [(s, n) for s in range(PACK)], half_done[y])
-                    mask_own_keys(half_done[y][:, n, 0:PACK, 3 * QUARTER : P], n)
-                if n == PACK - 1:
+                if n in (0, 6):
+                    c = 2 * y + 2 + n // 6
+                    if c < len(chunks):
+                        prepare_chunk(*chunks[c])
+                        later(STEPS * y + 8, quantise_v, *chunks[c])
+                        if c - 2 + LOADS_AHEAD < len(chunks):
+                            load_chunk(*chunks[c - 2 + LOADS_AHEAD])
+                t = n - 1
+                if 0 <= t < PACK:
+                    first_trip(h, r, [(s, t) for s in range(PACK)], half_done[y])
+                    mask_own_keys(half_done[y][:, t, 0:PACK, 3 * QUARTER : P], t)
+                if t == PACK - 1:
                     for s in (2, 3):
                         mask_own_keys(half_done[y][:, :, s, 2 * QUARTER : 3 * QUARTER], None)
-                if n == PACK:
+                if t == PACK:
                     first_trip(h, r, [(PACK, t) for t in range(PACK)], half_done[y])
                     for quarter in (1, 3):
                         own = slice(quarter * QUARTER, (quarter + 1) * QUARTER)
                         mask_own_keys(half_done[y][:, :, PACK, own], None)
-                if n in (5, 6):
-                    c = prepared + 2 * y + n - 5
-                    if c < len(chunks):
-                        prepare_chunk(*chunks[c])
-                        if c - prepared + LOADS_AHEAD < len(chunks):
-                            load_chunk(*chunks[c - prepared + LOADS_AHEAD])
-                if n in (9, 10):
-                    c = prepared + 2 * y + n - 9
-                    if c < len(chunks):
-                        quantise_v(*chunks[c])
-                if n >= STEPS - N_SETS:
-                    second_trip(h, n - (STEPS - N_SETS), half_done[y], packed[y])
+                s = n - (STEPS - N_SETS) + (2 if y == last else 0)
+                if 0 <= s < N_SETS:
+                    second_trip(h, s, half_done[y], packed[y])
+                    if s == PACK - 1:
+                        later(step + (1 if y == last else 3), quantise_sets, y, slice(0, PACK))
+                    if s == PACK:
+                        later(step + (1 if y == last else 3), quantise_sets, y, slice(PACK, N_SETS))
+                if n == 0 and y < last:
+                    for pos in range(2):
+                        when = step + STEPS + 6 + 2 * pos
+                        later(when, multiply_and_store, when, 1, y, h, r + pos)
+                if n == 0 and y == last:
+                    later(step + STEPS + 1, finish, y, h, r)
 
-            if y > 0:
-                h, r = pairs[y - 1]
-                if n == 0:
-                    quantise_sets(y - 1, slice(0, PACK))
-                if n == 1:
-                    quantise_sets(y - 1, slice(PACK, N_SETS))
-                if n in (5, 7):
-                    acc[n] = weighted_values(y - 1, h, r + (n - 5) // 2)
-                if n in (6, 9):
-                    store(h, r + (n - 6) // 3, acc[5 if n == 6 else 7])
-            if step in to_quantise:
-                quantise_scores(*to_quantise[step])
+            done = 0
+            while done < len(due.get(step, [])):
+                action, arguments = due[step][done]
+                action(*arguments)
+                done += 1

@@ -34,9 +34,15 @@ SETS = (
     ((0, 1, 0), (1, 1, 2 * QUARTER)),
 )
 N_SETS = len(SETS)
+KEY_COLUMN = (2, 2, 1, 1, 0)
 
-LOADS_AHEAD = 2 * N_CHUNKS
-STEPS = 12
+BLOCK_SLOTS = 12
+SLOTS = BLOCK_SLOTS + N_SETS
+
+LOADS_AHEAD = N_CHUNKS
+STEPS = BLOCK_SLOTS
+PAUSE = 2
+PIECES = 4
 
 FLOPS = 2 * 2 * HEADS * D * sum(CHUNK * CHUNK * (r + 1) for r in range(N_CHUNKS))
 
@@ -48,10 +54,10 @@ def tile_model_pa_kernel(tc, q_scaled, k, v, out):
     with ExitStack() as ctx:
         ctx.enter_context(tc.manual_schedule())
         const = ctx.enter_context(tc.tile_pool(name="const", bufs=1))
-        raw = ctx.enter_context(tc.tile_pool(name="raw", bufs=LOADS_AHEAD // N_CHUNKS + 2))
+        raw = ctx.enter_context(tc.tile_pool(name="raw", bufs=3))
         per_head = ctx.enter_context(tc.tile_pool(name="per_head", bufs=2))
-        per_chunk = ctx.enter_context(tc.tile_pool(name="per_chunk", bufs=5))
-        work = ctx.enter_context(tc.tile_pool(name="work", bufs=3))
+        per_pair = ctx.enter_context(tc.tile_pool(name="per_pair", bufs=3))
+        work = ctx.enter_context(tc.tile_pool(name="work", bufs=2))
         psum_vector = ctx.enter_context(tc.psum_pool(name="psum_vector", bufs=4))
         psum_scalar = ctx.enter_context(tc.psum_pool(name="psum_scalar", bufs=4))
 
@@ -98,12 +104,12 @@ def tile_model_pa_kernel(tc, q_scaled, k, v, out):
         make_identity(nc, identity[:])
         query_exponent = exponents([P, PACK], "query_exponent", [((every,), [[-1, PACK]], 0, 1)])
         key_exponent = exponents(
-            [P, N_SETS],
+            [P, 3],
             "key_exponent",
             [
-                ((slice(first, P), slice(s, s + 1)), [[0, 1]], P * b, -PACK)
-                for s in range(N_SETS)
-                for pos, b, first in SETS[s]
+                ((every,), [[P, 3]], P, -PACK),
+                ((slice(2 * QUARTER, P), slice(0, 1)), [[0, 1]], P, -PACK),
+                ((slice(3 * QUARTER, P), slice(1, 2)), [[0, 1]], 0, -PACK),
             ],
         )
         identity_f32 = const.tile([P, P], F32)
@@ -121,8 +127,8 @@ def tile_model_pa_kernel(tc, q_scaled, k, v, out):
                 tiles.append(zeroed)
 
         k_t, q_t, decay, query_factor, key_factor = {}, {}, {}, {}, {}
-        v_grouped, v_codes, v_scales, p_codes, p_scales = {}, {}, {}, {}, {}
-        half_done, packed, packed_codes, packed_scales = {}, {}, {}, {}
+        v_grouped, v_codes, v_scales = {}, {}, {}
+        half_done, p_grouped, p_codes, p_scales = {}, {}, {}, {}
 
         def power_of_gamma(h, exponent, label):
             power = per_head.tile(list(exponent.shape), F32, name=label)
@@ -168,34 +174,35 @@ def tile_model_pa_kernel(tc, q_scaled, k, v, out):
             )
 
         def quantise_v(h, c):
+            both = slice(c, c + 2)
             nc.vector.quantize_mx(
-                out=v_codes[h][:, c, :].bitcast(FP8X4),
-                scales=v_scales[h][:, c, :],
-                in_=v_grouped[h][:, c, :, :].rearrange("p d t -> p (d t)"),
+                out=v_codes[h][:, both, :].rearrange("p c d -> p (c d)").bitcast(FP8X4),
+                scales=v_scales[h][:, both, :].rearrange("p c d -> p (c d)"),
+                in_=v_grouped[h][:, both, :, :].rearrange("p c d t -> p (c d t)"),
             )
             n, two, three = h % 2, 2 * QUARTER, 3 * QUARTER
-            moves = [
-                (v_012[n][0:three, c, :], v_codes[h][0:three, c, :]),
-                (v_0[n][three:P, c, :], v_codes[h][0:QUARTER, c, :]),
-                (v_0_scales[n][three : three + 4, c, :], v_scales[h][0:4, c, :]),
-            ]
-            if c % 2 == 0:
-                moves += [(v_01[n][0:two, c, :], v_codes[h][0:two, c, :])]
-            else:
-                moves += [
-                    (v_01[n][two:P, c, :], v_codes[h][0:two, c, :]),
-                    (v_01_scales[n][two : two + 4, c, :], v_scales[h][0:4, c, :]),
-                    (v_01_scales[n][three : three + 4, c, :], v_scales[h][QUARTER : QUARTER + 4, c, :]),
-                ]
-            for target, source in moves:
+            even, odd = slice(c, c + 1), slice(c + 1, c + 2)
+            for target, source in (
+                (v_012[n][0:three, both, :], v_codes[h][0:three, both, :]),
+                (v_0[n][three:P, both, :], v_codes[h][0:QUARTER, both, :]),
+                (v_0_scales[n][three : three + 4, both, :], v_scales[h][0:4, both, :]),
+                (v_01[n][0:two, even, :], v_codes[h][0:two, even, :]),
+                (v_01[n][two:P, odd, :], v_codes[h][0:two, odd, :]),
+                (v_01_scales[n][two : two + 4, odd, :], v_scales[h][0:4, odd, :]),
+                (v_01_scales[n][three : three + 4, odd, :], v_scales[h][QUARTER : QUARTER + 4, odd, :]),
+            ):
                 nc.sync.dma_start(out=target.bitcast(I32), in_=source.bitcast(I32))
 
         def block(transposed, index):
             return transposed[:, index * P : (index + 1) * P]
 
 
-        def vector_block(h, r, g, b, grouped):
-            scores_t = psum_vector.tile([P, PACK, P], F32, name="scores_t")
+        def off_diagonal(y, slot, on_vector):
+            h, r, g, b = blocks[y][slot]
+            if on_vector:
+                scores_t = psum_vector.tile([P, PACK, P], F32, name="scores_t")
+            else:
+                scores_t = psum_scalar.tile([P, PACK, P], F32, tag="bank")
             for t in range(PACK):
                 nc.tensor.matmul(
                     out=scores_t[:, t, :],
@@ -204,15 +211,21 @@ def tile_model_pa_kernel(tc, q_scaled, k, v, out):
                     start=True,
                     stop=True,
                 )
-            distance = CHUNK * (r - g) + P * b
-            nc.vector.scalar_tensor_tensor(
-                out=grouped[:, b, :, :],
-                in0=scores_t[:].rearrange("p t i -> p i t"),
-                scalar=gammas[h] ** (distance - SHIFT),
-                in1=decay[h][:],
-                op0=MULT,
-                op1=MULT,
-            )
+            factor = gammas[h] ** (CHUNK * (r - g) + P * b - SHIFT)
+            in_order = scores_t[:].rearrange("p t i -> p i t")
+            p_block = p_grouped[y][:, slot, :, :]
+            if on_vector:
+                nc.vector.scalar_tensor_tensor(
+                    out=p_block, in0=in_order, scalar=factor, in1=decay[h][:], op0=MULT, op1=MULT
+                )
+            else:
+                scaled = work.tile([P, P, PACK], F32, name="scaled")
+                nc.scalar.activation(out=scaled[:], in_=in_order, func=COPY, scale=factor)
+                for piece in range(PIECES):
+                    part = slice(piece * P // PIECES, (piece + 1) * P // PIECES)
+                    nc.gpsimd.tensor_tensor(
+                        out=p_block[:, part, :], in0=scaled[:, part, :], in1=decay[h][:, part, :], op=MULT
+                    )
 
         def first_trip(h, r, columns, half_done):
             scores = psum_scalar.tile([P, PACK, P], F32, tag="bank")
@@ -249,42 +262,34 @@ def tile_model_pa_kernel(tc, q_scaled, k, v, out):
                 channel_multiplier=1,
             )
 
-        def second_trip(h, s, half_done, packed):
+        def second_trip(y, s, half_done):
+            h = pairs[y][0]
             flipped = psum_scalar.tile([P, PACK, P], F32, tag="bank")
             for t in range(PACK):
                 nc.tensor.transpose(out=flipped[:, t, :], in_=half_done[:, t, s, :], identity=identity_f32[:])
             nc.scalar.activation(
-                out=packed[:, s, :, :],
+                out=p_grouped[y][:, BLOCK_SLOTS + s, :, :],
                 in_=flipped[:].rearrange("p t i -> p i t"),
                 func=COPY,
-                scale=key_factor[h][:, s : s + 1],
+                scale=key_factor[h][:, KEY_COLUMN[s] : KEY_COLUMN[s] + 1],
             )
 
-        def quantise_scores(h, r, g, grouped, blocks):
-            if (h, r) not in p_codes:
-                p_codes[h, r] = per_chunk.tile([P, N_CHUNKS - 1, CHUNK], U32, name="p_codes", align_bytes=64)
-                p_scales[h, r] = per_chunk.tile([P, N_CHUNKS - 1, CHUNK], U8, name="p_scales", align_bytes=64)
+        def quantise_slots(y, slots):
+            if y not in p_codes:
+                p_codes[y] = per_pair.tile([P, SLOTS, P], U32, name="p_codes", align_bytes=64)
+                p_scales[y] = per_pair.tile([P, SLOTS, P], U8, name="p_scales", align_bytes=64)
             nc.vector.quantize_mx(
-                out=p_codes[h, r][:, g, blocks.start * P : blocks.stop * P].bitcast(FP8X4),
-                scales=p_scales[h, r][:, g, blocks.start * P : blocks.stop * P],
-                in_=grouped[:, blocks, :, :].rearrange("p b i t -> p (b i t)"),
-            )
-
-        def quantise_sets(y, sets):
-            if y not in packed_codes:
-                packed_codes[y] = work.tile([P, N_SETS, P], U32, name="packed_codes", align_bytes=64)
-                packed_scales[y] = work.tile([P, N_SETS, P], U8, name="packed_scales", align_bytes=64)
-            nc.vector.quantize_mx(
-                out=packed_codes[y][:, sets, :].rearrange("p s i -> p (s i)").bitcast(FP8X4),
-                scales=packed_scales[y][:, sets, :].rearrange("p s i -> p (s i)"),
-                in_=packed[y][:, sets, :, :].rearrange("p s i t -> p (s i t)"),
+                out=p_codes[y][:, slots, :].rearrange("p s i -> p (s i)").bitcast(FP8X4),
+                scales=p_scales[y][:, slots, :].rearrange("p s i -> p (s i)"),
+                in_=p_grouped[y][:, slots, :, :].rearrange("p s i t -> p (s i t)"),
             )
 
         def new_acc(blocks):
             return psum_scalar.tile([P, len(blocks), D], F32, name="acc", tag="bank")
 
-        def weighted_values(y, h, r, blocks, turns, acc):
+        def weighted_values(h, r, blocks, turns, acc):
             pos, n = r % 2, h % 2
+            y = pairs.index((h, r - pos))
             on_diagonal = {
                 3: (pos, v_codes[h], v_scales[h]),
                 2: (2 + pos, v_012[n], v_scales[h]),
@@ -293,18 +298,17 @@ def tile_model_pa_kernel(tc, q_scaled, k, v, out):
             }
             order = list(range(r - 1)) + [r] + list(range(max(r - 1, 0), r))
             for place, b in enumerate(blocks):
-                queries = slice(b * P, (b + 1) * P)
                 for g in order[turns]:
                     if g < r:
-                        codes, scales = p_codes[h, r][:, g, queries], p_scales[h, r][:, g, queries]
+                        of_pair, slot = slot_of[h, r, g, b]
                         values, value_scales = v_codes[h], v_scales[h]
                     else:
                         s, values, value_scales = on_diagonal[b]
-                        codes, scales = packed_codes[y][:, s, :], packed_scales[y][:, s, :]
+                        of_pair, slot = y, BLOCK_SLOTS + s
                     nc.tensor.matmul_mx(
                         out=acc[:, place, :],
-                        lhsT=codes.bitcast(FP8X4),
-                        lhsT_scale=scales,
+                        lhsT=p_codes[of_pair][:, slot, :].bitcast(FP8X4),
+                        lhsT_scale=p_scales[of_pair][:, slot, :],
                         rhs=values[:, g, :].bitcast(FP8X4),
                         rhs_scale=value_scales[:, g, :],
                         start=(g == order[0]),
@@ -319,9 +323,12 @@ def tile_model_pa_kernel(tc, q_scaled, k, v, out):
                 out=out[0, h, first : first + len(blocks) * P, :].rearrange("(b p) d -> p b d", p=P), in_=result[:]
             )
 
-        vector_blocks = [
-            (h, r, g, b) for h in range(HEADS) for r in range(N_CHUNKS) for g in range(r) for b in range(PACK)
-        ]
+        blocks, slot_of = [], {}
+        for y, (h, first) in enumerate(pairs):
+            of_pair = (1, 2) if first == 0 else (3,)
+            blocks.append([(h, r, g, b) for r in of_pair for g in range(r) for b in range(PACK)])
+            for slot, which in enumerate(blocks[y]):
+                slot_of[which] = (y, slot)
         last = len(pairs) - 1
         every_block = range(PACK)
         due = {}
@@ -329,20 +336,20 @@ def tile_model_pa_kernel(tc, q_scaled, k, v, out):
         def later(step, action, *arguments):
             due.setdefault(step, []).append((action, arguments))
 
-        def multiply_and_store(step, delay, y, h, r):
+        def multiply_and_store(step, h, r):
             acc = new_acc(every_block)
-            weighted_values(y, h, r, every_block, every, acc)
-            later(step + delay, store, h, r, every_block, acc, nc.scalar.copy)
+            weighted_values(h, r, every_block, every, acc)
+            later(step + 1, store, h, r, every_block, acc, nc.scalar.copy)
 
-        def finish(y, h, r):
+        def finish(h, r):
             accs = [new_acc([b]) for b in every_block]
             for b in every_block:
-                weighted_values(y, h, r + 1, [b], slice(0, r + 1), accs[b])
+                weighted_values(h, r + 1, [b], slice(0, r + 1), accs[b])
             acc = psum_vector.tile([P, PACK, D], F32, name="scores_t")
-            weighted_values(y, h, r, every_block, every, acc)
+            weighted_values(h, r, every_block, every, acc)
             store(h, r, every_block, acc, nc.scalar.copy)
             for b in every_block:
-                weighted_values(y, h, r + 1, [b], slice(r + 1, r + 2), accs[b])
+                weighted_values(h, r + 1, [b], slice(r + 1, r + 2), accs[b])
             for b in every_block:
                 store(h, r + 1, [b], accs[b], nc.vector.tensor_copy if b % 2 else nc.scalar.copy)
 
@@ -351,33 +358,25 @@ def tile_model_pa_kernel(tc, q_scaled, k, v, out):
         transpose_chunk("q", 0, 1)
         for c in range(2):
             group_v(0, c)
-            later(2 + c, quantise_v, 0, c)
+        later(2, quantise_v, 0, 0)
 
         for step in range(STEPS * (len(pairs) + 1)):
             y, n = divmod(step, STEPS)
-            if step < len(vector_blocks):
-                h, r, g, b = vector_blocks[step]
-                if b == 0:
-                    grouped = work.tile([P, PACK, P, PACK], BF16, name="grouped", bufs=4, align_bytes=64)
-                vector_block(h, r, g, b, grouped)
-                if step >= len(vector_blocks) - PACK:
-                    later(step + 1, quantise_scores, h, r, g, grouped, slice(b, b + 1))
-                elif b == PACK - 1:
-                    later(step + (1 + PACK if n < PACK else 1), quantise_scores, h, r, g, grouped, slice(0, PACK))
-
-            if step == 0:
-                transpose_chunk("q", 0, 0)
-                transpose_chunk("k", 0, 1)
             if y <= last:
                 h, r = pairs[y]
                 if n == 0:
-                    half_done[y] = work.tile([P, PACK, N_SETS, P], F32, name="half_done", bufs=2)
-                    packed[y] = work.tile([P, N_SETS, P, PACK], BF16, name="packed", bufs=2, align_bytes=64)
+                    half_done[y] = work.tile([P, PACK, N_SETS, P], F32, name="half_done")
+                    p_grouped[y] = work.tile([P, SLOTS, P, PACK], BF16, name="p_grouped", align_bytes=64)
+                off_diagonal(y, n, n != PAUSE)
+                if y == last and n >= 8:
+                    later(step + 1, quantise_slots, y, slice(n, n + 1))
+                if step == 0:
+                    transpose_chunk("q", 0, 0)
+                    transpose_chunk("k", 0, 1)
                 if n in (0, 6):
                     c = 2 * y + 2 + n // 6
                     if c < len(chunks):
                         prepare_chunk(*chunks[c])
-                        later(STEPS * y + 8, quantise_v, *chunks[c])
                         if c - 2 + LOADS_AHEAD < len(chunks):
                             load_chunk(*chunks[c - 2 + LOADS_AHEAD])
                 t = n - 1
@@ -394,17 +393,21 @@ def tile_model_pa_kernel(tc, q_scaled, k, v, out):
                         mask_own_keys(half_done[y][:, :, PACK, own], None)
                 s = n - (STEPS - N_SETS) + (2 if y == last else 0)
                 if 0 <= s < N_SETS:
-                    second_trip(h, s, half_done[y], packed[y])
-                    if s == PACK - 1:
-                        later(step + (1 if y == last else 3), quantise_sets, y, slice(0, PACK))
-                    if s == PACK:
-                        later(step + (1 if y == last else 3), quantise_sets, y, slice(PACK, N_SETS))
-                if n == 0 and y < last:
-                    for pos in range(2):
-                        when = step + STEPS + 6 + 2 * pos
-                        later(when, multiply_and_store, when, 1, y, h, r + pos)
-                if n == 0 and y == last:
-                    later(step + STEPS + 1, finish, y, h, r)
+                    second_trip(y, s, half_done[y])
+                if n == 0:
+                    later(step + 8, quantise_slots, y, slice(0, 8))
+                    if 2 * y + 2 < len(chunks):
+                        later(step + 8, quantise_v, *chunks[2 * y + 2])
+                    if y < last:
+                        later(step + STEPS + PAUSE, quantise_slots, y, slice(8, 16))
+                        later(step + STEPS + PAUSE, quantise_slots, y, slice(16, SLOTS))
+                        for pos in range(2):
+                            when = step + STEPS + 6 + 2 * pos
+                            later(when, multiply_and_store, when, h, r + pos)
+                    else:
+                        later(step + 9, quantise_slots, y, slice(BLOCK_SLOTS, BLOCK_SLOTS + PACK))
+                        later(step + 10, quantise_slots, y, slice(BLOCK_SLOTS + PACK, SLOTS))
+                        later(step + STEPS + 1, finish, h, r)
 
             done = 0
             while done < len(due.get(step, [])):

@@ -41,8 +41,6 @@ SLOTS = BLOCK_SLOTS + N_SETS
 
 LOADS_AHEAD = N_CHUNKS
 STEPS = BLOCK_SLOTS
-PAUSE = 2
-PIECES = 4
 
 FLOPS = 2 * 2 * HEADS * D * sum(CHUNK * CHUNK * (r + 1) for r in range(N_CHUNKS))
 
@@ -83,9 +81,11 @@ def tile_model_pa_kernel(tc, q_scaled, k, v, out):
         load("q", 0, 1)
         load("q", 0, 0)
         load("k", 0, 1)
-        load("v", 0, 0)
-        load("v", 0, 1)
-        for chunk in chunks[2:LOADS_AHEAD]:
+        load("k", 0, 2)
+        load("q", 0, 2)
+        for c in range(3):
+            load("v", 0, c)
+        for chunk in chunks[3:LOADS_AHEAD]:
             load_chunk(*chunk)
 
         def exponents(shape, label, pieces):
@@ -142,6 +142,8 @@ def tile_model_pa_kernel(tc, q_scaled, k, v, out):
             v_codes[h] = per_head.tile([P, N_CHUNKS, D], U32, name="v_codes", align_bytes=64)
             v_scales[h] = per_head.tile([P, N_CHUNKS, D], U8, name="v_scales", align_bytes=64)
             decay[h] = power_of_gamma(h, table_exponent, "decay")
+
+        def scalar_factors(h):
             query_factor[h] = power_of_gamma(h, query_exponent, "query_factor")
             key_factor[h] = power_of_gamma(h, key_exponent, "key_factor")
 
@@ -159,18 +161,14 @@ def tile_model_pa_kernel(tc, q_scaled, k, v, out):
         def prepare_chunk(h, c):
             if c == 0:
                 start_head(h)
+                scalar_factors(h)
             transpose_chunk("k", h, c)
             transpose_chunk("q", h, c)
-            group_v(h, c)
 
         def group_v(h, c):
-            nc.gpsimd.tensor_scalar(
+            nc.scalar.copy(
                 out=v_grouped[h][:, c, :, :],
-                in0=rows["v", h][:, PACK * c : PACK * (c + 1), :].rearrange("p t d -> p d t"),
-                scalar1=1.0,
-                scalar2=0.0,
-                op0=MULT,
-                op1=mybir.AluOpType.add,
+                in_=rows["v", h][:, PACK * c : PACK * (c + 1), :].rearrange("p t d -> p d t"),
             )
 
         def quantise_v(h, c):
@@ -197,12 +195,9 @@ def tile_model_pa_kernel(tc, q_scaled, k, v, out):
             return transposed[:, index * P : (index + 1) * P]
 
 
-        def off_diagonal(y, slot, on_vector):
+        def vector_block(y, slot):
             h, r, g, b = blocks[y][slot]
-            if on_vector:
-                scores_t = psum_vector.tile([P, PACK, P], F32, name="scores_t")
-            else:
-                scores_t = psum_scalar.tile([P, PACK, P], F32, tag="bank")
+            scores_t = psum_vector.tile([P, PACK, P], F32, name="scores_t")
             for t in range(PACK):
                 nc.tensor.matmul(
                     out=scores_t[:, t, :],
@@ -211,21 +206,15 @@ def tile_model_pa_kernel(tc, q_scaled, k, v, out):
                     start=True,
                     stop=True,
                 )
-            factor = gammas[h] ** (CHUNK * (r - g) + P * b - SHIFT)
-            in_order = scores_t[:].rearrange("p t i -> p i t")
-            p_block = p_grouped[y][:, slot, :, :]
-            if on_vector:
-                nc.vector.scalar_tensor_tensor(
-                    out=p_block, in0=in_order, scalar=factor, in1=decay[h][:], op0=MULT, op1=MULT
-                )
-            else:
-                scaled = work.tile([P, P, PACK], F32, name="scaled")
-                nc.scalar.activation(out=scaled[:], in_=in_order, func=COPY, scale=factor)
-                for piece in range(PIECES):
-                    part = slice(piece * P // PIECES, (piece + 1) * P // PIECES)
-                    nc.gpsimd.tensor_tensor(
-                        out=p_block[:, part, :], in0=scaled[:, part, :], in1=decay[h][:, part, :], op=MULT
-                    )
+            distance = CHUNK * (r - g) + P * b
+            nc.vector.scalar_tensor_tensor(
+                out=p_grouped[y][:, slot, :, :],
+                in0=scores_t[:].rearrange("p t i -> p i t"),
+                scalar=gammas[h] ** (distance - SHIFT),
+                in1=decay[h][:],
+                op0=MULT,
+                op1=MULT,
+            )
 
         def first_trip(h, r, columns, half_done):
             scores = psum_scalar.tile([P, PACK, P], F32, tag="bank")
@@ -344,21 +333,16 @@ def tile_model_pa_kernel(tc, q_scaled, k, v, out):
         def finish(h, r):
             accs = [new_acc([b]) for b in every_block]
             for b in every_block:
-                weighted_values(h, r + 1, [b], slice(0, r + 1), accs[b])
-            acc = psum_vector.tile([P, PACK, D], F32, name="scores_t")
-            weighted_values(h, r, every_block, every, acc)
-            store(h, r, every_block, acc, nc.scalar.copy)
+                weighted_values(h, r, [b], slice(0, r), accs[b])
             for b in every_block:
-                weighted_values(h, r + 1, [b], slice(r + 1, r + 2), accs[b])
+                weighted_values(h, r, [b], slice(r, r + 1), accs[b])
             for b in every_block:
-                store(h, r + 1, [b], accs[b], nc.vector.tensor_copy if b % 2 else nc.scalar.copy)
+                store(h, r, [b], accs[b], nc.vector.tensor_copy if b % 2 else nc.scalar.copy)
 
         start_head(0)
         transpose_chunk("k", 0, 0)
         transpose_chunk("q", 0, 1)
-        for c in range(2):
-            group_v(0, c)
-        later(2, quantise_v, 0, 0)
+        scalar_factors(0)
 
         for step in range(STEPS * (len(pairs) + 1)):
             y, n = divmod(step, STEPS)
@@ -367,13 +351,13 @@ def tile_model_pa_kernel(tc, q_scaled, k, v, out):
                 if n == 0:
                     half_done[y] = work.tile([P, PACK, N_SETS, P], F32, name="half_done")
                     p_grouped[y] = work.tile([P, SLOTS, P, PACK], BF16, name="p_grouped", align_bytes=64)
-                off_diagonal(y, n, n != PAUSE)
+                vector_block(y, n)
                 if y == last and n >= 8:
                     later(step + 1, quantise_slots, y, slice(n, n + 1))
                 if step == 0:
                     transpose_chunk("q", 0, 0)
                     transpose_chunk("k", 0, 1)
-                if n in (0, 6):
+                if n in (2 if y == 0 else 0, 6):
                     c = 2 * y + 2 + n // 6
                     if c < len(chunks):
                         prepare_chunk(*chunks[c])
@@ -391,23 +375,25 @@ def tile_model_pa_kernel(tc, q_scaled, k, v, out):
                     for quarter in (1, 3):
                         own = slice(quarter * QUARTER, (quarter + 1) * QUARTER)
                         mask_own_keys(half_done[y][:, :, PACK, own], None)
-                s = n - (STEPS - N_SETS) + (2 if y == last else 0)
-                if 0 <= s < N_SETS:
-                    second_trip(y, s, half_done[y])
+                for s in range(N_SETS):
+                    if n == (6 + s // 2 if y == last else STEPS - N_SETS + s):
+                        second_trip(y, s, half_done[y])
                 if n == 0:
+                    later(step + 4, group_v, *chunks[2 * y])
+                    later(step + 5, group_v, *chunks[2 * y + 1])
+                    later(step + 7, quantise_v, *chunks[2 * y])
                     later(step + 8, quantise_slots, y, slice(0, 8))
-                    if 2 * y + 2 < len(chunks):
-                        later(step + 8, quantise_v, *chunks[2 * y + 2])
                     if y < last:
-                        later(step + STEPS + PAUSE, quantise_slots, y, slice(8, 16))
-                        later(step + STEPS + PAUSE, quantise_slots, y, slice(16, SLOTS))
+                        later(step + STEPS + 2, quantise_slots, y, slice(8, 16))
+                        later(step + STEPS + 2, quantise_slots, y, slice(16, SLOTS))
                         for pos in range(2):
                             when = step + STEPS + 6 + 2 * pos
                             later(when, multiply_and_store, when, h, r + pos)
                     else:
                         later(step + 9, quantise_slots, y, slice(BLOCK_SLOTS, BLOCK_SLOTS + PACK))
-                        later(step + 10, quantise_slots, y, slice(BLOCK_SLOTS + PACK, SLOTS))
-                        later(step + STEPS + 1, finish, h, r)
+                        later(step + 9, quantise_slots, y, slice(BLOCK_SLOTS + PACK, SLOTS))
+                        later(step + 11, multiply_and_store, step + 11, h, r)
+                        later(step + STEPS + 1, finish, h, r + 1)
 
             done = 0
             while done < len(due.get(step, [])):

@@ -167,8 +167,8 @@ def tile_model_pa_kernel(tc, q_scaled, k, v, out):
 
         def group_v(h, c):
             nc.scalar.copy(
-                out=v_grouped[h][:, c, :, :],
-                in_=rows["v", h][:, PACK * c : PACK * (c + 1), :].rearrange("p t d -> p d t"),
+                out=v_grouped[h][:, c, :, :].rearrange("p (d e) t -> p d t e", e=PACK),
+                in_=rows["v", h][:, PACK * c : PACK * (c + 1), :].rearrange("p t (d e) -> p d t e", e=PACK),
             )
 
         def quantise_v(h, c):

import math
from contextlib import ExitStack

import concourse.mybir as mybir
from concourse.masks import make_identity

BF16 = mybir.dt.bfloat16
F32 = mybir.dt.float32
I32 = mybir.dt.int32
U32 = mybir.dt.uint32
U8 = mybir.dt.uint8
FP8X4 = mybir.dt.float8_e4m3fn_x4
MULT = mybir.AluOpType.mult
COPY = mybir.ActivationFunctionType.Copy
EXP = mybir.ActivationFunctionType.Exp

HEADS = 8
SEQ = 2048
D = 128
P = 128
PACK = 4
CHUNK = P * PACK
N_CHUNKS = SEQ // CHUNK
BLOCKS = SEQ // P
QUARTER = P // PACK

SHIFT = CHUNK - 1

SETS = (
    ((0, 3, 0),),
    ((1, 3, 0),),
    ((0, 2, 0), (0, 0, 3 * QUARTER)),
    ((1, 2, 0), (1, 0, 3 * QUARTER)),
    ((0, 1, 0), (1, 1, 2 * QUARTER)),
)
N_SETS = len(SETS)
KEY_COLUMN = (2, 2, 1, 1, 0)

BLOCK_SLOTS = 12
SLOTS = BLOCK_SLOTS + N_SETS

LOADS_AHEAD = N_CHUNKS
STEPS = BLOCK_SLOTS

FLOPS = 2 * 2 * HEADS * D * sum(CHUNK * CHUNK * (r + 1) for r in range(N_CHUNKS))


def tile_model_pa_kernel(tc, q_scaled, k, v, out):
    nc = tc.nc
    gammas = [1.0 - 2.0 ** (-5 - h) for h in range(HEADS)]

    with ExitStack() as ctx:
        ctx.enter_context(tc.manual_schedule())
        const = ctx.enter_context(tc.tile_pool(name="const", bufs=1))
        raw = ctx.enter_context(tc.tile_pool(name="raw", bufs=3))
        per_head = ctx.enter_context(tc.tile_pool(name="per_head", bufs=2))
        per_pair = ctx.enter_context(tc.tile_pool(name="per_pair", bufs=3))
        work = ctx.enter_context(tc.tile_pool(name="work", bufs=2))
        psum_vector = ctx.enter_context(tc.psum_pool(name="psum_vector", bufs=4))
        psum_scalar = ctx.enter_context(tc.psum_pool(name="psum_scalar", bufs=4))

        sources = {"k": (k, "(p b) d -> p b d"), "q": (q_scaled, "(b p) d -> p b d"), "v": (v, "(p b) d -> p b d")}
        rows = {}

        def load(which, h, c):
            if (which, h) not in rows:
                rows[which, h] = raw.tile([P, BLOCKS, D], BF16, name=which + "_raw")
            source, order = sources[which]
            nc.sync.dma_start(
                out=rows[which, h][:, PACK * c : PACK * (c + 1), :],
                in_=source[0, h, CHUNK * c : CHUNK * (c + 1), :].rearrange(order, p=P),
            )

        def load_chunk(h, c):
            for which in ("k", "q", "v"):
                load(which, h, c)

        chunks = [(h, r) for h in range(HEADS) for r in range(N_CHUNKS)]
        pairs = [(h, r) for h in range(HEADS) for r in range(0, N_CHUNKS, 2)]
        load("k", 0, 0)
        load("q", 0, 1)
        load("q", 0, 0)
        load("k", 0, 1)
        load("k", 0, 2)
        load("q", 0, 2)
        for c in range(3):
            load("v", 0, c)
        for chunk in chunks[3:LOADS_AHEAD]:
            load_chunk(*chunk)

        def exponents(shape, label, pieces):
            as_i32 = const.tile(shape, I32, name=label + "_i32")
            for part, pattern, base, channel_multiplier in pieces:
                nc.gpsimd.iota(as_i32[part], pattern=pattern, base=base, channel_multiplier=channel_multiplier)
            as_f32 = const.tile(shape, F32, name=label)
            nc.vector.tensor_copy(out=as_f32[:], in_=as_i32[:])
            return as_f32

        every = slice(None)
        table_exponent = exponents(
            [P, P, PACK], "table_exponent", [((every,), [[1, P], [-1, PACK]], SHIFT, -PACK)]
        )
        identity = const.tile([P, P], BF16)
        make_identity(nc, identity[:])
        query_exponent = exponents([P, PACK], "query_exponent", [((every,), [[-1, PACK]], 0, 1)])
        key_exponent = exponents(
            [P, 3],
            "key_exponent",
            [
                ((every,), [[P, 3]], P, -PACK),
                ((slice(2 * QUARTER, P), slice(0, 1)), [[0, 1]], P, -PACK),
                ((slice(3 * QUARTER, P), slice(1, 2)), [[0, 1]], 0, -PACK),
            ],
        )
        identity_f32 = const.tile([P, P], F32)
        make_identity(nc, identity_f32[:])

        v_012, v_0, v_01, v_0_scales, v_01_scales = [], [], [], [], []
        for parity in range(2):
            for tiles, label in ((v_012, "v_012"), (v_0, "v_0"), (v_01, "v_01")):
                zeroed = const.tile([P, N_CHUNKS, D], U32, name="%s_%d" % (label, parity), align_bytes=64)
                nc.vector.memset(zeroed[:], 0)
                tiles.append(zeroed)
            for tiles, label in ((v_0_scales, "v_0_scales"), (v_01_scales, "v_01_scales")):
                zeroed = const.tile([P, N_CHUNKS, D], U8, name="%s_%d" % (label, parity), align_bytes=64)
                nc.vector.memset(zeroed[:].bitcast(I32), 0)
                tiles.append(zeroed)

        k_t, q_t, decay, query_factor, key_factor = {}, {}, {}, {}, {}
        v_grouped, v_codes, v_scales = {}, {}, {}
        half_done, p_grouped, p_codes, p_scales = {}, {}, {}, {}

        def power_of_gamma(h, exponent, label):
            power = per_head.tile(list(exponent.shape), F32, name=label)
            nc.scalar.activation(out=power[:], in_=exponent[:], func=EXP, scale=math.log(gammas[h]))
            return power

        def start_head(h):
            k_t[h] = per_head.tile([P, SEQ], BF16, name="k_t")
            q_t[h] = per_head.tile([P, SEQ], BF16, name="q_t")
            v_grouped[h] = per_head.tile([P, N_CHUNKS, D, PACK], BF16, name="v_grouped", align_bytes=64)
            v_codes[h] = per_head.tile([P, N_CHUNKS, D], U32, name="v_codes", align_bytes=64)
            v_scales[h] = per_head.tile([P, N_CHUNKS, D], U8, name="v_scales", align_bytes=64)
            decay[h] = power_of_gamma(h, table_exponent, "decay")

        def scalar_factors(h):
            query_factor[h] = power_of_gamma(h, query_exponent, "query_factor")
            key_factor[h] = power_of_gamma(h, key_exponent, "key_factor")

        def transpose_chunk(which, h, c):
            transposed = (k_t if which == "k" else q_t)[h]
            flipped = psum_scalar.tile([P, PACK, P], BF16, tag="bank")
            for b in range(PACK):
                nc.tensor.transpose(
                    out=flipped[:, b, :], in_=rows[which, h][:, PACK * c + b, :], identity=identity[:]
                )
            nc.scalar.copy(
                out=transposed[:, c * CHUNK : (c + 1) * CHUNK], in_=flipped[:].rearrange("p b x -> p (b x)")
            )

        def prepare_chunk(h, c):
            if c == 0:
                start_head(h)
                scalar_factors(h)
            transpose_chunk("k", h, c)
            transpose_chunk("q", h, c)

        def group_v(h, c):
            nc.scalar.copy(
                out=v_grouped[h][:, c, :, :].rearrange("p (d e) t -> p d t e", e=PACK),
                in_=rows["v", h][:, PACK * c : PACK * (c + 1), :].rearrange("p t (d e) -> p d t e", e=PACK),
            )

        def quantise_v(h, c):
            both = slice(c, c + 2)
            nc.vector.quantize_mx(
                out=v_codes[h][:, both, :].rearrange("p c d -> p (c d)").bitcast(FP8X4),
                scales=v_scales[h][:, both, :].rearrange("p c d -> p (c d)"),
                in_=v_grouped[h][:, both, :, :].rearrange("p c d t -> p (c d t)"),
            )
            n, two, three = h % 2, 2 * QUARTER, 3 * QUARTER
            even, odd = slice(c, c + 1), slice(c + 1, c + 2)
            for target, source in (
                (v_012[n][0:three, both, :], v_codes[h][0:three, both, :]),
                (v_0[n][three:P, both, :], v_codes[h][0:QUARTER, both, :]),
                (v_0_scales[n][three : three + 4, both, :], v_scales[h][0:4, both, :]),
                (v_01[n][0:two, even, :], v_codes[h][0:two, even, :]),
                (v_01[n][two:P, odd, :], v_codes[h][0:two, odd, :]),
                (v_01_scales[n][two : two + 4, odd, :], v_scales[h][0:4, odd, :]),
                (v_01_scales[n][three : three + 4, odd, :], v_scales[h][QUARTER : QUARTER + 4, odd, :]),
            ):
                nc.sync.dma_start(out=target.bitcast(I32), in_=source.bitcast(I32))

        def block(transposed, index):
            return transposed[:, index * P : (index + 1) * P]


        def vector_block(y, slot):
            h, r, g, b = blocks[y][slot]
            scores_t = psum_vector.tile([P, PACK, P], F32, name="scores_t")
            for t in range(PACK):
                nc.tensor.matmul(
                    out=scores_t[:, t, :],
                    lhsT=block(k_t[h], PACK * g + t),
                    rhs=block(q_t[h], PACK * r + b),
                    start=True,
                    stop=True,
                )
            distance = CHUNK * (r - g) + P * b
            nc.vector.scalar_tensor_tensor(
                out=p_grouped[y][:, slot, :, :],
                in0=scores_t[:].rearrange("p t i -> p i t"),
                scalar=gammas[h] ** (distance - SHIFT),
                in1=decay[h][:],
                op0=MULT,
                op1=MULT,
            )

        def first_trip(h, r, columns, half_done):
            scores = psum_scalar.tile([P, PACK, P], F32, tag="bank")
            for place, (s, t) in enumerate(columns):
                for pos, b, first in SETS[s]:
                    words = QUARTER * (b + 1)
                    nc.tensor.matmul(
                        out=scores[:, place, first : first + words],
                        lhsT=block(q_t[h], PACK * (r + pos) + b),
                        rhs=block(k_t[h], PACK * (r + pos) + t)[:, 0:words],
                        start=True,
                        stop=True,
                    )
            place = 0
            while place < PACK:
                s, t = columns[place]
                alike = len([c for c in columns if c[1] == t])
                nc.scalar.activation(
                    out=half_done[:, t, s : s + alike, :],
                    in_=scores[:, place : place + alike, :],
                    func=COPY,
                    scale=query_factor[h][:, t : t + 1],
                )
                place += alike

        def mask_own_keys(own, t):
            nc.gpsimd.affine_select(
                out=own,
                in_=own,
                pattern=[[-1 if t is None else 0, own.shape[1]], [-PACK, QUARTER]],
                compare_op=mybir.AluOpType.is_ge,
                fill=0.0,
                base=0 if t is None else -t,
                channel_multiplier=1,
            )

        def second_trip(y, s, half_done):
            h = pairs[y][0]
            flipped = psum_scalar.tile([P, PACK, P], F32, tag="bank")
            for t in range(PACK):
                nc.tensor.transpose(out=flipped[:, t, :], in_=half_done[:, t, s, :], identity=identity_f32[:])
            nc.scalar.activation(
                out=p_grouped[y][:, BLOCK_SLOTS + s, :, :],
                in_=flipped[:].rearrange("p t i -> p i t"),
                func=COPY,
                scale=key_factor[h][:, KEY_COLUMN[s] : KEY_COLUMN[s] + 1],
            )

        def quantise_slots(y, slots):
            if y not in p_codes:
                p_codes[y] = per_pair.tile([P, SLOTS, P], U32, name="p_codes", align_bytes=64)
                p_scales[y] = per_pair.tile([P, SLOTS, P], U8, name="p_scales", align_bytes=64)
            nc.vector.quantize_mx(
                out=p_codes[y][:, slots, :].rearrange("p s i -> p (s i)").bitcast(FP8X4),
                scales=p_scales[y][:, slots, :].rearrange("p s i -> p (s i)"),
                in_=p_grouped[y][:, slots, :, :].rearrange("p s i t -> p (s i t)"),
            )

        def new_acc(blocks):
            return psum_scalar.tile([P, len(blocks), D], F32, name="acc", tag="bank")

        def weighted_values(h, r, blocks, turns, acc):
            pos, n = r % 2, h % 2
            y = pairs.index((h, r - pos))
            on_diagonal = {
                3: (pos, v_codes[h], v_scales[h]),
                2: (2 + pos, v_012[n], v_scales[h]),
                1: (4, v_01[n], v_01_scales[n] if pos else v_scales[h]),
                0: (2 + pos, v_0[n], v_0_scales[n]),
            }
            order = list(range(r - 1)) + [r] + list(range(max(r - 1, 0), r))
            for place, b in enumerate(blocks):
                for g in order[turns]:
                    if g < r:
                        of_pair, slot = slot_of[h, r, g, b]
                        values, value_scales = v_codes[h], v_scales[h]
                    else:
                        s, values, value_scales = on_diagonal[b]
                        of_pair, slot = y, BLOCK_SLOTS + s
                    nc.tensor.matmul_mx(
                        out=acc[:, place, :],
                        lhsT=p_codes[of_pair][:, slot, :].bitcast(FP8X4),
                        lhsT_scale=p_scales[of_pair][:, slot, :],
                        rhs=values[:, g, :].bitcast(FP8X4),
                        rhs_scale=value_scales[:, g, :],
                        start=(g == order[0]),
                        stop=(g == order[-1]),
                    )

        def store(h, r, blocks, acc, copy):
            result = work.tile([P, len(blocks), D], F32, name="result", bufs=6)
            copy(out=result[:], in_=acc[:])
            first = r * CHUNK + blocks[0] * P
            nc.sync.dma_start(
                out=out[0, h, first : first + len(blocks) * P, :].rearrange("(b p) d -> p b d", p=P), in_=result[:]
            )

        blocks, slot_of = [], {}
        for y, (h, first) in enumerate(pairs):
            of_pair = (1, 2) if first == 0 else (3,)
            blocks.append([(h, r, g, b) for r in of_pair for g in range(r) for b in range(PACK)])
            for slot, which in enumerate(blocks[y]):
                slot_of[which] = (y, slot)
        last = len(pairs) - 1
        every_block = range(PACK)
        due = {}

        def later(step, action, *arguments):
            due.setdefault(step, []).append((action, arguments))

        def multiply_and_store(step, h, r):
            acc = new_acc(every_block)
            weighted_values(h, r, every_block, every, acc)
            later(step + 1, store, h, r, every_block, acc, nc.scalar.copy)

        def finish(h, r):
            accs = [new_acc([b]) for b in every_block]
            for b in every_block:
                weighted_values(h, r, [b], slice(0, r), accs[b])
            for b in every_block:
                weighted_values(h, r, [b], slice(r, r + 1), accs[b])
            for b in every_block:
                store(h, r, [b], accs[b], nc.vector.tensor_copy if b % 2 else nc.scalar.copy)

        start_head(0)
        transpose_chunk("k", 0, 0)
        transpose_chunk("q", 0, 1)
        scalar_factors(0)

        for step in range(STEPS * (len(pairs) + 1)):
            y, n = divmod(step, STEPS)
            if y <= last:
                h, r = pairs[y]
                if n == 0:
                    half_done[y] = work.tile([P, PACK, N_SETS, P], F32, name="half_done")
                    p_grouped[y] = work.tile([P, SLOTS, P, PACK], BF16, name="p_grouped", align_bytes=64)
                vector_block(y, n)
                if y == last and n >= 8:
                    later(step + 1, quantise_slots, y, slice(n, n + 1))
                if step == 0:
                    transpose_chunk("q", 0, 0)
                    transpose_chunk("k", 0, 1)
                if n in (2 if y == 0 else 0, 6):
                    c = 2 * y + 2 + n // 6
                    if c < len(chunks):
                        prepare_chunk(*chunks[c])
                        if c - 2 + LOADS_AHEAD < len(chunks):
                            load_chunk(*chunks[c - 2 + LOADS_AHEAD])
                t = n - 1
                if 0 <= t < PACK:
                    first_trip(h, r, [(s, t) for s in range(PACK)], half_done[y])
                    mask_own_keys(half_done[y][:, t, 0:PACK, 3 * QUARTER : P], t)
                if t == PACK - 1:
                    for s in (2, 3):
                        mask_own_keys(half_done[y][:, :, s, 2 * QUARTER : 3 * QUARTER], None)
                if t == PACK:
                    first_trip(h, r, [(PACK, t) for t in range(PACK)], half_done[y])
                    for quarter in (1, 3):
                        own = slice(quarter * QUARTER, (quarter + 1) * QUARTER)
                        mask_own_keys(half_done[y][:, :, PACK, own], None)
                for s in range(N_SETS):
                    if n == (6 + s // 2 if y == last else STEPS - N_SETS + s):
                        second_trip(y, s, half_done[y])
                if n == 0:
                    later(step + 4, group_v, *chunks[2 * y])
                    later(step + 5, group_v, *chunks[2 * y + 1])
                    later(step + 7, quantise_v, *chunks[2 * y])
                    later(step + 8, quantise_slots, y, slice(0, 8))
                    if y < last:
                        later(step + STEPS + 2, quantise_slots, y, slice(8, 16))
                        later(step + STEPS + 2, quantise_slots, y, slice(16, SLOTS))
                        for pos in range(2):
                            when = step + STEPS + 6 + 2 * pos
                            later(when, multiply_and_store, when, h, r + pos)
                    else:
                        later(step + 9, quantise_slots, y, slice(BLOCK_SLOTS, BLOCK_SLOTS + PACK))
                        later(step + 9, quantise_slots, y, slice(BLOCK_SLOTS + PACK, SLOTS))
                        later(step + 11, multiply_and_store, step + 11, h, r)
                        later(step + STEPS + 1, finish, h, r + 1)

            done = 0
            while done < len(due.get(step, [])):
                action, arguments = due[step][done]
                action(*arguments)
                done += 1
